import numpy as np
import ml_dtypes


def mxq(x, axis, fmt="e4m3"):
    dtype, down = {"e4m3": (ml_dtypes.float8_e4m3fn, 7), "e5m2": (ml_dtypes.float8_e5m2, 14)}[fmt]
    v = np.moveaxis(np.asarray(x, np.float32).astype(ml_dtypes.bfloat16).astype(np.float64), axis, -1)
    blocks = v.reshape(v.shape[:-1] + (-1, 32))
    amax = np.abs(blocks).max(-1, keepdims=True)
    byte = np.maximum(np.where(amax > 0, np.frexp(amax)[1] - 1 + 127, 0) - down, 1)
    scale = np.exp2(byte - 127.0)
    codes = (blocks / scale).astype(np.float32).astype(dtype).astype(np.float64)
    return np.moveaxis((codes * scale).reshape(v.shape), -1, axis)


WIDE = False


def mx_kscale(k):
    if not WIDE:
        return np.ones(k)
    levels = np.array([10, -10, 5, -5, 0])
    a = np.random.permutation(np.resize(levels, k // 512 * 4)).reshape(k // 512, 4)
    idx = np.arange(k)
    return np.exp2(a[idx // 512, idx % 128 // 32])


BF16 = ml_dtypes.bfloat16


def bf(x):
    return np.asarray(x, np.float32).astype(BF16)


def f64(x):
    return np.asarray(x).astype(np.float64)


B, T, D, O = 16, 32, 16384, 512


def erf(z):
    a = np.clip(z, -6.0, 6.0)
    q = 2.0 * a * a
    term = a.copy()
    total = a.copy()
    for k in range(1, 130):
        term = term * q / (2 * k + 1)
        total = total + term
    return 2.0 / np.sqrt(np.pi) * np.exp(-a * a) * total


def gelu_exact(v):
    return 0.5 * v * (1.0 + erf(v / np.sqrt(2.0)))


def setup_inputs():
    s = mx_kscale(D)
    x = np.random.standard_normal((B, T, D)) * s
    lengths = np.random.randint(T // 4, T + 1, size=B)
    lengths[np.random.randint(B)] = T
    pad = np.arange(T)[None, :] >= lengths[:, None]
    x = np.where(pad[:, :, None], -1.0, x)
    return {"x": bf(x), "W": bf(np.random.standard_normal((O, D)) / np.sqrt(D) / s[None, :]), "b": bf(np.random.standard_normal(O) * 0.3)}


def reference(x, W, b):
    x = f64(x)
    valid = ~np.all(x == -1.0, axis=-1)
    y = gelu_exact((mxq(x, 2, "e4m3") @ mxq(f64(W), 1, "e4m3").T) + f64(b))
    vf = valid[..., None].astype(np.float64)
    n = np.sum(vf, axis=1)
    mean = np.sum(y * vf, axis=1) / n
    diff = (y - mean[:, None, :]) * vf
    var = np.sum(diff * diff, axis=1) / np.maximum(n - 1.0, 1.0)
    std = np.where(n > 1.0, np.sqrt(var), np.zeros_like(var))
    out = np.concatenate([std, mean], axis=-1)
    return np.where(np.isnan(out), np.zeros_like(out), out)

@@ -1,0 +1,258 @@
+from contextlib import ExitStack
+
+import concourse.mybir as mybir
+from concourse.masks import make_identity
+
+F32 = mybir.dt.float32
+BF16 = mybir.dt.bfloat16
+U32 = mybir.dt.uint32
+U8 = mybir.dt.uint8
+FP8X4 = mybir.dt.float8_e4m3fn_x4
+ALU = mybir.AluOpType
+ACT = mybir.ActivationFunctionType
+AX = mybir.AxisListType
+
+P = 128
+SAMPLES, TOKENS, D, O = 16, 32, 16384, 512
+ROWS = SAMPLES * TOKENS
+ROW_TILES = ROWS // P
+K_PASS = 4 * P
+WORDS_PASS = K_PASS // 2
+ROUNDS = D // K_PASS
+
+CHUNK_MAX = 4 * K_PASS
+CHUNK_WIDTHS = [K_PASS, K_PASS, 2 * K_PASS] + [CHUNK_MAX] * (D // CHUNK_MAX - 1)
+CHUNKS_AHEAD = 4
+
+PAD_WORD = -(1.0 + 49024.0 / 8388608.0)
+SQRT_FLOOR = 2.0 ** -100
+
+FLOPS = 2 * ROWS * O * D
+
+
+def tile_linearnnencoder_k_kernel(tc, x, W, b, out):
+    nc = tc.nc
+    assert sum(CHUNK_WIDTHS) == D
+
+    x_rows = x.rearrange("s t k -> (s t) k").rearrange("(a p) k -> p a k", p=P)
+    w_rows = W.rearrange("(a p) k -> p a k", p=P)
+
+    with ExitStack() as ctx:
+        ctx.enter_context(tc.manual_schedule())
+        const = ctx.enter_context(tc.tile_pool(name="const", bufs=1))
+        natural = ctx.enter_context(tc.tile_pool(name="natural", bufs=CHUNKS_AHEAD))
+        grouped = ctx.enter_context(tc.tile_pool(name="grouped", bufs=3))
+        packed = ctx.enter_context(tc.tile_pool(name="packed", bufs=3))
+        scratch = ctx.enter_context(tc.tile_pool(name="scratch", bufs=4))
+        tail = ctx.enter_context(tc.tile_pool(name="tail", bufs=2))
+        acc_pool = ctx.enter_context(tc.psum_pool(name="acc", bufs=1))
+        flip_pool = ctx.enter_context(tc.psum_pool(name="flip", bufs=1))
+
+        chunk_start = [sum(CHUNK_WIDTHS[:c]) for c in range(len(CHUNK_WIDTHS))]
+        chunk_tiles = {}
+
+        def load_chunk(c):
+            k0, width = chunk_start[c], CHUNK_WIDTHS[c]
+            x_nat = natural.tile([P, ROW_TILES, CHUNK_MAX], BF16, name="x_nat")
+            nc.sync.dma_start(out=x_nat[:, :, :width], in_=x_rows[:, :, k0 : k0 + width])
+            w_nat = natural.tile([P, ROW_TILES, CHUNK_MAX], BF16, name="w_nat")
+            nc.sync.dma_start(out=w_nat[:, :, :width], in_=w_rows[:, :, k0 : k0 + width])
+            chunk_tiles[c] = (x_nat, w_nat)
+
+        def as_words(nat):
+            flat = nat[:].rearrange("p a k -> p (a k)").bitcast(F32)
+            return flat.rearrange("p (a w) -> p a w", a=ROW_TILES)
+
+        for c in range(CHUNKS_AHEAD):
+            load_chunk(c)
+
+        ident = const.tile([P, P], F32, name="ident")
+        make_identity(nc, ident[:])
+
+        b_rows = const.tile([P, P], BF16, name="b_rows")
+        nc.vector.memset(b_rows[:], 0.0)
+        nc.scalar.dma_start(out=b_rows[0:ROW_TILES, :], in_=b.rearrange("(m o) -> m o", o=P))
+        b_rows32 = const.tile([P, P], F32, name="b_rows32")
+        nc.vector.tensor_copy(out=b_rows32[:], in_=b_rows[:])
+
+        one = const.tile([P, 1], F32, name="one")
+        nc.vector.memset(one[:], 1.0)
+        warm = const.tile([P, 2], F32, name="warm")
+        nc.scalar.activation(out=warm[:, 0:1], in_=one[:], func=ACT.Gelu)
+
+        differing = const.tile([P, ROW_TILES, len(CHUNK_WIDTHS)], F32, name="differing")
+
+        acc = [acc_pool.tile([P, ROWS], F32, name="acc%d" % m) for m in range(ROW_TILES)]
+
+        def flip_rows(words, word0, label):
+            banks = []
+            for half in range(2):
+                bank = flip_pool.tile([P, 2, 2, P], F32, name="%s_flip%d" % (label, half))
+                for i in range(2):
+                    for u in range(2):
+                        first = word0 + P * u
+                        nc.tensor.transpose(
+                            bank[:, i, u, :], words[:, 2 * half + i, first : first + P], ident[:]
+                        )
+                banks.append(bank)
+            return banks
+
+        def gather_words(banks, label):
+            rows4 = grouped.tile([P, 4 * ROWS], BF16, name="%s_rows4" % label, align_bytes=64)
+            by_row = rows4[:].bitcast(F32).rearrange("p (a r u) -> p a r u", a=ROW_TILES, u=2)
+            for half in range(2):
+                nc.scalar.copy(
+                    out=by_row[:, 2 * half : 2 * half + 2, :, :],
+                    in_=banks[half][:].rearrange("p i u r -> p i r u"),
+                )
+            return rows4
+
+        def quantise(rows4, label):
+            codes = packed.tile([P, ROWS], U32, name="%s_codes" % label, align_bytes=64)
+            scales = packed.tile([P, ROWS], U8, name="%s_scales" % label, align_bytes=64)
+            nc.vector.quantize_mx(out=codes[:].bitcast(FP8X4), scales=scales[:], in_=rows4[:])
+            return codes, scales
+
+        def multiply(operands, r):
+            (x_codes, x_scales), (w_codes, w_scales) = operands
+            for m in range(ROW_TILES):
+                cols = slice(P * m, P * (m + 1))
+                nc.tensor.matmul_mx(
+                    out=acc[m][:],
+                    lhsT=w_codes[:, cols].bitcast(FP8X4),
+                    lhsT_scale=w_scales[:, cols],
+                    rhs=x_codes[:].bitcast(FP8X4),
+                    rhs_scale=x_scales[:],
+                    start=(r == 0),
+                    stop=(r == ROUNDS - 1),
+                )
+
+        def test_padding(words, c, a):
+            n_words = CHUNK_WIDTHS[c] // 2
+            unequal = scratch.tile([P, CHUNK_MAX // 2], BF16, name="unequal")
+            nc.vector.tensor_scalar(
+                out=unequal[:, :n_words],
+                in0=words[:, a, :n_words],
+                scalar1=PAD_WORD,
+                scalar2=None,
+                op0=ALU.not_equal,
+                op1=ALU.add,
+                accum_out=differing[:, a, c : c + 1],
+            )
+
+        def find_valid_tokens():
+            total = const.tile([P, ROW_TILES], F32, name="total")
+            nc.vector.tensor_reduce(out=total[:], in_=differing[:], axis=AX.X, op=ALU.add)
+            valid_col = const.tile([P, ROW_TILES], F32, name="valid_col")
+            nc.vector.tensor_single_scalar(out=valid_col[:], in_=total[:], scalar=0.0, op=ALU.is_gt)
+            return valid_col
+
+        waiting = None
+        r = 0
+        for c in range(len(CHUNK_WIDTHS)):
+            x_words = as_words(chunk_tiles[c][0])
+            w_words = as_words(chunk_tiles[c][1])
+            rounds_here = CHUNK_WIDTHS[c] // K_PASS
+            tests_a_round = ROW_TILES // rounds_here
+            for j in range(rounds_here):
+                x_banks = flip_rows(x_words, WORDS_PASS * j, "x")
+                w_banks = flip_rows(w_words, WORDS_PASS * j, "w")
+                x_rows4 = gather_words(x_banks, "x")
+                w_rows4 = gather_words(w_banks, "w")
+                if waiting is not None:
+                    multiply(waiting, r - 1)
+                for a in range(tests_a_round * j, tests_a_round * (j + 1)):
+                    test_padding(x_words, c, a)
+                if r == ROUNDS - 1:
+                    valid_col = find_valid_tokens()
+                waiting = (quantise(x_rows4, "x"), quantise(w_rows4, "w"))
+                r += 1
+            if c + CHUNKS_AHEAD < len(CHUNK_WIDTHS):
+                load_chunk(c + CHUNKS_AHEAD)
+
+        b_flip = flip_pool.tile([P, P], F32, name="b_flip", tag="x_flip1")
+        nc.tensor.transpose(b_flip[:], b_rows32[:], ident[:])
+        valid_bank = flip_pool.tile([P, ROWS], F32, name="valid_bank", tag="x_flip0")
+        for a in range(ROW_TILES):
+            nc.tensor.matmul(
+                out=valid_bank[:, P * a : P * (a + 1)],
+                lhsT=valid_col[:, a : a + 1].to_broadcast([P, P]),
+                rhs=ident[:],
+                start=True,
+                stop=True,
+            )
+        multiply(waiting, ROUNDS - 1)
+
+        bias_col = const.tile([P, ROW_TILES], F32, name="bias_col")
+        nc.vector.tensor_copy(out=bias_col[:], in_=b_flip[:, 0:ROW_TILES])
+        valid = const.tile([P, SAMPLES, TOKENS], F32, name="valid")
+        nc.vector.tensor_copy(out=valid[:].rearrange("p s t -> p (s t)"), in_=valid_bank[:])
+        n_valid = const.tile([P, SAMPLES], F32, name="n_valid")
+        nc.vector.tensor_reduce(out=n_valid[:], in_=valid[:], axis=AX.X, op=ALU.add)
+        n_floor = const.tile([P, 2, SAMPLES], F32, name="n_floor")
+        nc.vector.tensor_scalar_max(out=n_floor[:, 0, :], in0=n_valid[:], scalar1=1.0)
+        nc.vector.tensor_scalar(
+            out=n_floor[:, 1, :], in0=n_valid[:], scalar1=-1.0, scalar2=1.0, op0=ALU.add, op1=ALU.max
+        )
+        n_inverse = const.tile([P, 2, SAMPLES], F32, name="n_inverse")
+        nc.vector.reciprocal(out=n_inverse[:], in_=n_floor[:])
+
+        stats = const.tile([P, SAMPLES, 2, ROW_TILES], F32, name="stats")
+        variance = const.tile([P, SAMPLES, ROW_TILES], F32, name="variance")
+        shape = [P, SAMPLES, TOKENS]
+
+        y = []
+        for m in range(ROW_TILES):
+            y_m = tail.tile(shape, F32, name="y%d" % m, bufs=1)
+            nc.scalar.activation(
+                out=y_m[:].rearrange("p s t -> p (s t)"),
+                in_=acc[m][:],
+                func=ACT.Gelu,
+                bias=bias_col[:, m : m + 1],
+            )
+            y.append(y_m)
+        nc.scalar.activation(out=warm[:, 1:2], in_=one[:], func=ACT.Sqrt)
+
+        def sum_of_squares(squares, m):
+            total_sq = tail.tile([P, SAMPLES], F32, name="total_sq")
+            nc.vector.tensor_reduce(out=total_sq[:], in_=squares[:], axis=AX.X, op=ALU.add)
+            nc.vector.scalar_tensor_tensor(
+                out=variance[:, :, m],
+                in0=total_sq[:],
+                scalar=SQRT_FLOOR,
+                in1=n_inverse[:, 1, :],
+                op0=ALU.max,
+                op1=ALU.mult,
+            )
+
+        squares = [None] * ROW_TILES
+        for m in range(ROW_TILES):
+            kept = tail.tile(shape, F32, name="kept")
+            nc.vector.tensor_tensor(out=kept[:], in0=y[m][:], in1=valid[:], op=ALU.mult)
+            total_y = tail.tile([P, SAMPLES], F32, name="total_y")
+            nc.vector.tensor_reduce(out=total_y[:], in_=kept[:], axis=AX.X, op=ALU.add)
+            mean = stats[:, :, 1, m]
+            nc.vector.tensor_tensor(out=mean, in0=total_y[:], in1=n_inverse[:, 0, :], op=ALU.mult)
+            away = tail.tile(shape, F32, name="away")
+            nc.vector.tensor_tensor(
+                out=away[:], in0=y[m][:], in1=mean.unsqueeze(2).to_broadcast(shape), op=ALU.subtract
+            )
+            away_kept = tail.tile(shape, F32, name="away_kept")
+            nc.vector.tensor_tensor(out=away_kept[:], in0=away[:], in1=valid[:], op=ALU.mult)
+            squares[m] = tail.tile(shape, F32, name="squares")
+            nc.scalar.activation(out=squares[m][:], in_=away_kept[:], func=ACT.Square)
+            if m > 0:
+                sum_of_squares(squares[m - 1], m - 1)
+        sum_of_squares(squares[ROW_TILES - 1], ROW_TILES - 1)
+
+        root = const.tile([P, SAMPLES, ROW_TILES], F32, name="root")
+        nc.scalar.activation(out=root[:], in_=variance[:], func=ACT.Sqrt)
+        some = const.tile([P, SAMPLES, ROW_TILES], F32, name="some")
+        nc.vector.tensor_single_scalar(out=some[:], in_=variance[:], scalar=SQRT_FLOOR, op=ALU.is_gt)
+        nc.vector.tensor_tensor(out=stats[:, :, 0, :], in0=root[:], in1=some[:], op=ALU.mult)
+
+        stats_bank = flip_pool.tile([P, P], F32, name="stats_bank", tag="w_flip0")
+        nc.tensor.transpose(stats_bank[:], stats[:].rearrange("p s g m -> p (s g m)"), ident[:])
+        result = const.tile([P, P], F32, name="result")
+        nc.vector.tensor_copy(out=result[:], in_=stats_bank[:])
+        nc.sync.dma_start(out=out.rearrange("s (g o) -> (s g) o", o=P), in_=result[:])

@@ -21,8 +21,10 @@ WORDS_PASS = K_PASS // 2
 ROUNDS = D // K_PASS
 
 CHUNK_MAX = 4 * K_PASS
-CHUNK_WIDTHS = [K_PASS, K_PASS, 2 * K_PASS] + [CHUNK_MAX] * (D // CHUNK_MAX - 1)
-CHUNKS_AHEAD = 4
+CHUNK_WIDTHS = [K_PASS] * 4 + [2 * K_PASS] * 2 + [CHUNK_MAX] * (D // CHUNK_MAX - 2)
+CHUNKS_AHEAD = 3
+
+HELD = 16
 
 PAD_WORD = -(1.0 + 49024.0 / 8388608.0)
 SQRT_FLOOR = 2.0 ** -100
@@ -41,8 +43,9 @@ def tile_linearnnencoder_k_kernel(tc, x, W, b, out):
         ctx.enter_context(tc.manual_schedule())
         const = ctx.enter_context(tc.tile_pool(name="const", bufs=1))
         natural = ctx.enter_context(tc.tile_pool(name="natural", bufs=CHUNKS_AHEAD))
-        grouped = ctx.enter_context(tc.tile_pool(name="grouped", bufs=3))
+        grouped = ctx.enter_context(tc.tile_pool(name="grouped", bufs=2))
         packed = ctx.enter_context(tc.tile_pool(name="packed", bufs=3))
+        packed_held = ctx.enter_context(tc.tile_pool(name="packed_held", bufs=HELD))
         scratch = ctx.enter_context(tc.tile_pool(name="scratch", bufs=4))
         tail = ctx.enter_context(tc.tile_pool(name="tail", bufs=2))
         acc_pool = ctx.enter_context(tc.psum_pool(name="acc", bufs=1))
@@ -107,25 +110,25 @@ def tile_linearnnencoder_k_kernel(tc, x, W, b, out):
                 )
             return rows4
 
-        def quantise(rows4, label):
-            codes = packed.tile([P, ROWS], U32, name="%s_codes" % label, align_bytes=64)
-            scales = packed.tile([P, ROWS], U8, name="%s_scales" % label, align_bytes=64)
-            nc.vector.quantize_mx(out=codes[:].bitcast(FP8X4), scales=scales[:], in_=rows4[:])
+        def quantise(rows4, n_rows, pool, label):
+            codes = pool.tile([P, n_rows], U32, name="%s_codes" % label, align_bytes=64)
+            scales = pool.tile([P, n_rows], U8, name="%s_scales" % label, align_bytes=64)
+            nc.vector.quantize_mx(out=codes[:].bitcast(FP8X4), scales=scales[:], in_=rows4)
             return codes, scales
 
-        def multiply(operands, r):
-            (x_codes, x_scales), (w_codes, w_scales) = operands
-            for m in range(ROW_TILES):
-                cols = slice(P * m, P * (m + 1))
-                nc.tensor.matmul_mx(
-                    out=acc[m][:],
-                    lhsT=w_codes[:, cols].bitcast(FP8X4),
-                    lhsT_scale=w_scales[:, cols],
-                    rhs=x_codes[:].bitcast(FP8X4),
-                    rhs_scale=x_scales[:],
-                    start=(r == 0),
-                    stop=(r == ROUNDS - 1),
-                )
+        def multiply(operands, r, m):
+            x_codes, x_scales = operands[0]
+            w_codes, w_scales = operands[1 + m // 2]
+            cols = slice(P * (m % 2), P * (m % 2 + 1))
+            nc.tensor.matmul_mx(
+                out=acc[m][:],
+                lhsT=w_codes[:, cols].bitcast(FP8X4),
+                lhsT_scale=w_scales[:, cols],
+                rhs=x_codes[:].bitcast(FP8X4),
+                rhs_scale=x_scales[:],
+                start=(r == 0),
+                stop=(r == ROUNDS - 1),
+            )
 
         def test_padding(words, c, a):
             n_words = CHUNK_WIDTHS[c] // 2
@@ -148,6 +151,7 @@ def tile_linearnnencoder_k_kernel(tc, x, W, b, out):
             return valid_col
 
         waiting = None
+        held = []
         r = 0
         for c in range(len(CHUNK_WIDTHS)):
             x_words = as_words(chunk_tiles[c][0])
@@ -160,12 +164,22 @@ def tile_linearnnencoder_k_kernel(tc, x, W, b, out):
                 x_rows4 = gather_words(x_banks, "x")
                 w_rows4 = gather_words(w_banks, "w")
                 if waiting is not None:
-                    multiply(waiting, r - 1)
+                    multiply(waiting, r - 1, 0)
+                    multiply(waiting, r - 1, 1)
+                    if r - 1 < ROUNDS - HELD:
+                        multiply(waiting, r - 1, 2)
+                        multiply(waiting, r - 1, 3)
+                    else:
+                        held.append((waiting, r - 1))
                 for a in range(tests_a_round * j, tests_a_round * (j + 1)):
                     test_padding(x_words, c, a)
                 if r == ROUNDS - 1:
                     valid_col = find_valid_tokens()
-                waiting = (quantise(x_rows4, "x"), quantise(w_rows4, "w"))
+                waiting = (
+                    quantise(x_rows4[:], ROWS, packed_held, "x"),
+                    quantise(w_rows4[:, : 2 * ROWS], ROWS // 2, packed, "w_low"),
+                    quantise(w_rows4[:, 2 * ROWS :], ROWS // 2, packed_held, "w_high"),
+                )
                 r += 1
             if c + CHUNKS_AHEAD < len(CHUNK_WIDTHS):
                 load_chunk(c + CHUNKS_AHEAD)
@@ -181,12 +195,17 @@ def tile_linearnnencoder_k_kernel(tc, x, W, b, out):
                 start=True,
                 stop=True,
             )
-        multiply(waiting, ROUNDS - 1)
+        multiply(waiting, ROUNDS - 1, 0)
+        multiply(waiting, ROUNDS - 1, 1)
+        held.append((waiting, ROUNDS - 1))
+        for m in (2, 3):
+            for operands, held_round in held:
+                multiply(operands, held_round, m)
 
         bias_col = const.tile([P, ROW_TILES], F32, name="bias_col")
-        nc.vector.tensor_copy(out=bias_col[:], in_=b_flip[:, 0:ROW_TILES])
+        nc.scalar.copy(out=bias_col[:], in_=b_flip[:, 0:ROW_TILES])
         valid = const.tile([P, SAMPLES, TOKENS], F32, name="valid")
-        nc.vector.tensor_copy(out=valid[:].rearrange("p s t -> p (s t)"), in_=valid_bank[:])
+        nc.scalar.copy(out=valid[:].rearrange("p s t -> p (s t)"), in_=valid_bank[:])
         n_valid = const.tile([P, SAMPLES], F32, name="n_valid")
         nc.vector.tensor_reduce(out=n_valid[:], in_=valid[:], axis=AX.X, op=ALU.add)
         n_floor = const.tile([P, 2, SAMPLES], F32, name="n_floor")
@@ -202,7 +221,8 @@ def tile_linearnnencoder_k_kernel(tc, x, W, b, out):
         shape = [P, SAMPLES, TOKENS]
 
         y = []
-        for m in range(ROW_TILES):
+
+        def gelu(m):
             y_m = tail.tile(shape, F32, name="y%d" % m, bufs=1)
             nc.scalar.activation(
                 out=y_m[:].rearrange("p s t -> p (s t)"),
@@ -211,7 +231,9 @@ def tile_linearnnencoder_k_kernel(tc, x, W, b, out):
                 bias=bias_col[:, m : m + 1],
             )
             y.append(y_m)
-        nc.scalar.activation(out=warm[:, 1:2], in_=one[:], func=ACT.Sqrt)
+
+        gelu(0)
+        gelu(1)
 
         def sum_of_squares(squares, m):
             total_sq = tail.tile([P, SAMPLES], F32, name="total_sq")
@@ -241,6 +263,10 @@ def tile_linearnnencoder_k_kernel(tc, x, W, b, out):
             nc.vector.tensor_tensor(out=away_kept[:], in0=away[:], in1=valid[:], op=ALU.mult)
             squares[m] = tail.tile(shape, F32, name="squares")
             nc.scalar.activation(out=squares[m][:], in_=away_kept[:], func=ACT.Square)
+            if m + 2 < ROW_TILES:
+                gelu(m + 2)
+            if m + 2 == ROW_TILES - 1:
+                nc.scalar.activation(out=warm[:, 1:2], in_=one[:], func=ACT.Sqrt)
             if m > 0:
                 sum_of_squares(squares[m - 1], m - 1)
         sum_of_squares(squares[ROW_TILES - 1], ROW_TILES - 1)

@@ -24,7 +24,10 @@ CHUNK_MAX = 4 * K_PASS
 CHUNK_WIDTHS = [K_PASS] * 4 + [2 * K_PASS] * 2 + [CHUNK_MAX] * (D // CHUNK_MAX - 2)
 CHUNKS_AHEAD = 3
 
-HELD = 16
+PASS_LAG = 2
+
+HELD_TILE = ROW_TILES - 1
+HELD = 24
 
 PAD_WORD = -(1.0 + 49024.0 / 8388608.0)
 SQRT_FLOOR = 2.0 ** -100
@@ -44,9 +47,9 @@ def tile_linearnnencoder_k_kernel(tc, x, W, b, out):
         const = ctx.enter_context(tc.tile_pool(name="const", bufs=1))
         natural = ctx.enter_context(tc.tile_pool(name="natural", bufs=CHUNKS_AHEAD))
         grouped = ctx.enter_context(tc.tile_pool(name="grouped", bufs=2))
-        packed = ctx.enter_context(tc.tile_pool(name="packed", bufs=3))
+        packed = ctx.enter_context(tc.tile_pool(name="packed", bufs=PASS_LAG + 2))
         packed_held = ctx.enter_context(tc.tile_pool(name="packed_held", bufs=HELD))
-        scratch = ctx.enter_context(tc.tile_pool(name="scratch", bufs=4))
+        scratch = ctx.enter_context(tc.tile_pool(name="scratch", bufs=2))
         tail = ctx.enter_context(tc.tile_pool(name="tail", bufs=2))
         acc_pool = ctx.enter_context(tc.psum_pool(name="acc", bufs=1))
         flip_pool = ctx.enter_context(tc.psum_pool(name="flip", bufs=1))
@@ -118,12 +121,11 @@ def tile_linearnnencoder_k_kernel(tc, x, W, b, out):
 
         def multiply(operands, r, m):
             x_codes, x_scales = operands[0]
-            w_codes, w_scales = operands[1 + m // 2]
-            cols = slice(P * (m % 2), P * (m % 2 + 1))
+            w_codes, w_scales = operands[1 + m]
             nc.tensor.matmul_mx(
                 out=acc[m][:],
-                lhsT=w_codes[:, cols].bitcast(FP8X4),
-                lhsT_scale=w_scales[:, cols],
+                lhsT=w_codes[:].bitcast(FP8X4),
+                lhsT_scale=w_scales[:],
                 rhs=x_codes[:].bitcast(FP8X4),
                 rhs_scale=x_scales[:],
                 start=(r == 0),
@@ -150,8 +152,12 @@ def tile_linearnnencoder_k_kernel(tc, x, W, b, out):
             nc.vector.tensor_single_scalar(out=valid_col[:], in_=total[:], scalar=0.0, op=ALU.is_gt)
             return valid_col
 
-        waiting = None
-        held = []
+        def multiply_round(r):
+            for m in range(ROW_TILES):
+                if m != HELD_TILE or r < ROUNDS - HELD:
+                    multiply(quantised[r], r, m)
+
+        quantised = []
         r = 0
         for c in range(len(CHUNK_WIDTHS)):
             x_words = as_words(chunk_tiles[c][0])
@@ -163,26 +169,29 @@ def tile_linearnnencoder_k_kernel(tc, x, W, b, out):
                 w_banks = flip_rows(w_words, WORDS_PASS * j, "w")
                 x_rows4 = gather_words(x_banks, "x")
                 w_rows4 = gather_words(w_banks, "w")
-                if waiting is not None:
-                    multiply(waiting, r - 1, 0)
-                    multiply(waiting, r - 1, 1)
-                    if r - 1 < ROUNDS - HELD:
-                        multiply(waiting, r - 1, 2)
-                        multiply(waiting, r - 1, 3)
-                    else:
-                        held.append((waiting, r - 1))
+                if r >= PASS_LAG:
+                    multiply_round(r - PASS_LAG)
                 for a in range(tests_a_round * j, tests_a_round * (j + 1)):
                     test_padding(x_words, c, a)
                 if r == ROUNDS - 1:
                     valid_col = find_valid_tokens()
-                waiting = (
-                    quantise(x_rows4[:], ROWS, packed_held, "x"),
-                    quantise(w_rows4[:, : 2 * ROWS], ROWS // 2, packed, "w_low"),
-                    quantise(w_rows4[:, 2 * ROWS :], ROWS // 2, packed_held, "w_high"),
-                )
+                operands = [quantise(x_rows4[:], ROWS, packed_held, "x")]
+                for m in range(ROW_TILES):
+                    operands.append(
+                        quantise(
+                            w_rows4[:, 4 * P * m : 4 * P * (m + 1)],
+                            P,
+                            packed_held if m == HELD_TILE else packed,
+                            "w%d" % m,
+                        )
+                    )
+                quantised.append(operands)
                 r += 1
             if c + CHUNKS_AHEAD < len(CHUNK_WIDTHS):
                 load_chunk(c + CHUNKS_AHEAD)
+
+        for late_round in range(ROUNDS - PASS_LAG, ROUNDS - 1):
+            multiply_round(late_round)
 
         b_flip = flip_pool.tile([P, P], F32, name="b_flip", tag="x_flip1")
         nc.tensor.transpose(b_flip[:], b_rows32[:], ident[:])
@@ -195,12 +204,9 @@ def tile_linearnnencoder_k_kernel(tc, x, W, b, out):
                 start=True,
                 stop=True,
             )
-        multiply(waiting, ROUNDS - 1, 0)
-        multiply(waiting, ROUNDS - 1, 1)
-        held.append((waiting, ROUNDS - 1))
-        for m in (2, 3):
-            for operands, held_round in held:
-                multiply(operands, held_round, m)
+        multiply_round(ROUNDS - 1)
+        for held_round in range(ROUNDS - HELD, ROUNDS):
+            multiply(quantised[held_round], held_round, HELD_TILE)
 
         bias_col = const.tile([P, ROW_TILES], F32, name="bias_col")
         nc.scalar.copy(out=bias_col[:], in_=b_flip[:, 0:ROW_TILES])
@@ -232,8 +238,8 @@ def tile_linearnnencoder_k_kernel(tc, x, W, b, out):
             )
             y.append(y_m)
 
-        gelu(0)
-        gelu(1)
+        for m in range(HELD_TILE):
+            gelu(m)
 
         def sum_of_squares(squares, m):
             total_sq = tail.tile([P, SAMPLES], F32, name="total_sq")
@@ -263,9 +269,8 @@ def tile_linearnnencoder_k_kernel(tc, x, W, b, out):
             nc.vector.tensor_tensor(out=away_kept[:], in0=away[:], in1=valid[:], op=ALU.mult)
             squares[m] = tail.tile(shape, F32, name="squares")
             nc.scalar.activation(out=squares[m][:], in_=away_kept[:], func=ACT.Square)
-            if m + 2 < ROW_TILES:
-                gelu(m + 2)
-            if m + 2 == ROW_TILES - 1:
+            if m == HELD_TILE - 2:
+                gelu(HELD_TILE)
                 nc.scalar.activation(out=warm[:, 1:2], in_=one[:], func=ACT.Sqrt)
             if m > 0:
                 sum_of_squares(squares[m - 1], m - 1)

from contextlib import ExitStack

import concourse.mybir as mybir
from concourse.masks import make_identity

F32 = mybir.dt.float32
BF16 = mybir.dt.bfloat16
U32 = mybir.dt.uint32
U8 = mybir.dt.uint8
FP8X4 = mybir.dt.float8_e4m3fn_x4
ALU = mybir.AluOpType
ACT = mybir.ActivationFunctionType
AX = mybir.AxisListType

P = 128
SAMPLES, TOKENS, D, O = 16, 32, 16384, 512
ROWS = SAMPLES * TOKENS
ROW_TILES = ROWS // P
K_PASS = 4 * P
WORDS_PASS = K_PASS // 2
ROUNDS = D // K_PASS

CHUNK_MAX = 4 * K_PASS
CHUNK_WIDTHS = [K_PASS] * 4 + [2 * K_PASS] * 2 + [CHUNK_MAX] * (D // CHUNK_MAX - 2)
CHUNKS_AHEAD = 3

PASS_LAG = 2

HELD_TILE = ROW_TILES - 1
HELD = 24

PAD_WORD = -(1.0 + 49024.0 / 8388608.0)
SQRT_FLOOR = 2.0 ** -100

FLOPS = 2 * ROWS * O * D


def tile_linearnnencoder_k_kernel(tc, x, W, b, out):
    nc = tc.nc
    assert sum(CHUNK_WIDTHS) == D

    x_rows = x.rearrange("s t k -> (s t) k").rearrange("(a p) k -> p a k", p=P)
    w_rows = W.rearrange("(a p) k -> p a k", p=P)

    with ExitStack() as ctx:
        ctx.enter_context(tc.manual_schedule())
        const = ctx.enter_context(tc.tile_pool(name="const", bufs=1))
        natural = ctx.enter_context(tc.tile_pool(name="natural", bufs=CHUNKS_AHEAD))
        grouped = ctx.enter_context(tc.tile_pool(name="grouped", bufs=2))
        packed = ctx.enter_context(tc.tile_pool(name="packed", bufs=PASS_LAG + 2))
        packed_held = ctx.enter_context(tc.tile_pool(name="packed_held", bufs=HELD))
        scratch = ctx.enter_context(tc.tile_pool(name="scratch", bufs=2))
        tail = ctx.enter_context(tc.tile_pool(name="tail", bufs=2))
        acc_pool = ctx.enter_context(tc.psum_pool(name="acc", bufs=1))
        flip_pool = ctx.enter_context(tc.psum_pool(name="flip", bufs=1))

        chunk_start = [sum(CHUNK_WIDTHS[:c]) for c in range(len(CHUNK_WIDTHS))]
        chunk_tiles = {}

        def load_chunk(c):
            k0, width = chunk_start[c], CHUNK_WIDTHS[c]
            x_nat = natural.tile([P, ROW_TILES, CHUNK_MAX], BF16, name="x_nat")
            nc.sync.dma_start(out=x_nat[:, :, :width], in_=x_rows[:, :, k0 : k0 + width])
            w_nat = natural.tile([P, ROW_TILES, CHUNK_MAX], BF16, name="w_nat")
            nc.sync.dma_start(out=w_nat[:, :, :width], in_=w_rows[:, :, k0 : k0 + width])
            chunk_tiles[c] = (x_nat, w_nat)

        def as_words(nat):
            flat = nat[:].rearrange("p a k -> p (a k)").bitcast(F32)
            return flat.rearrange("p (a w) -> p a w", a=ROW_TILES)

        for c in range(CHUNKS_AHEAD):
            load_chunk(c)

        ident = const.tile([P, P], F32, name="ident")
        make_identity(nc, ident[:])

        b_rows = const.tile([P, P], BF16, name="b_rows")
        nc.vector.memset(b_rows[:], 0.0)
        nc.scalar.dma_start(out=b_rows[0:ROW_TILES, :], in_=b.rearrange("(m o) -> m o", o=P))
        b_rows32 = const.tile([P, P], F32, name="b_rows32")
        nc.vector.tensor_copy(out=b_rows32[:], in_=b_rows[:])

        one = const.tile([P, 1], F32, name="one")
        nc.vector.memset(one[:], 1.0)
        warm = const.tile([P, 2], F32, name="warm")
        nc.scalar.activation(out=warm[:, 0:1], in_=one[:], func=ACT.Gelu)

        differing = const.tile([P, ROW_TILES, len(CHUNK_WIDTHS)], F32, name="differing")

        acc = [acc_pool.tile([P, ROWS], F32, name="acc%d" % m) for m in range(ROW_TILES)]

        def flip_rows(words, word0, label):
            banks = []
            for half in range(2):
                bank = flip_pool.tile([P, 2, 2, P], F32, name="%s_flip%d" % (label, half))
                for i in range(2):
                    for u in range(2):
                        first = word0 + P * u
                        nc.tensor.transpose(
                            bank[:, i, u, :], words[:, 2 * half + i, first : first + P], ident[:]
                        )
                banks.append(bank)
            return banks

        def gather_words(banks, label):
            rows4 = grouped.tile([P, 4 * ROWS], BF16, name="%s_rows4" % label, align_bytes=64)
            by_row = rows4[:].bitcast(F32).rearrange("p (a r u) -> p a r u", a=ROW_TILES, u=2)
            for half in range(2):
                nc.scalar.copy(
                    out=by_row[:, 2 * half : 2 * half + 2, :, :],
                    in_=banks[half][:].rearrange("p i u r -> p i r u"),
                )
            return rows4

        def quantise(rows4, n_rows, pool, label):
            codes = pool.tile([P, n_rows], U32, name="%s_codes" % label, align_bytes=64)
            scales = pool.tile([P, n_rows], U8, name="%s_scales" % label, align_bytes=64)
            nc.vector.quantize_mx(out=codes[:].bitcast(FP8X4), scales=scales[:], in_=rows4)
            return codes, scales

        def multiply(operands, r, m):
            x_codes, x_scales = operands[0]
            w_codes, w_scales = operands[1 + m]
            nc.tensor.matmul_mx(
                out=acc[m][:],
                lhsT=w_codes[:].bitcast(FP8X4),
                lhsT_scale=w_scales[:],
                rhs=x_codes[:].bitcast(FP8X4),
                rhs_scale=x_scales[:],
                start=(r == 0),
                stop=(r == ROUNDS - 1),
            )

        def test_padding(words, c, a):
            n_words = CHUNK_WIDTHS[c] // 2
            unequal = scratch.tile([P, CHUNK_MAX // 2], BF16, name="unequal")
            nc.vector.tensor_scalar(
                out=unequal[:, :n_words],
                in0=words[:, a, :n_words],
                scalar1=PAD_WORD,
                scalar2=None,
                op0=ALU.not_equal,
                op1=ALU.add,
                accum_out=differing[:, a, c : c + 1],
            )

        def find_valid_tokens():
            total = const.tile([P, ROW_TILES], F32, name="total")
            nc.vector.tensor_reduce(out=total[:], in_=differing[:], axis=AX.X, op=ALU.add)
            valid_col = const.tile([P, ROW_TILES], F32, name="valid_col")
            nc.vector.tensor_single_scalar(out=valid_col[:], in_=total[:], scalar=0.0, op=ALU.is_gt)
            return valid_col

        def multiply_round(r):
            for m in range(ROW_TILES):
                if m != HELD_TILE or r < ROUNDS - HELD:
                    multiply(quantised[r], r, m)

        quantised = []
        r = 0
        for c in range(len(CHUNK_WIDTHS)):
            x_words = as_words(chunk_tiles[c][0])
            w_words = as_words(chunk_tiles[c][1])
            rounds_here = CHUNK_WIDTHS[c] // K_PASS
            tests_a_round = ROW_TILES // rounds_here
            for j in range(rounds_here):
                x_banks = flip_rows(x_words, WORDS_PASS * j, "x")
                w_banks = flip_rows(w_words, WORDS_PASS * j, "w")
                x_rows4 = gather_words(x_banks, "x")
                w_rows4 = gather_words(w_banks, "w")
                if r >= PASS_LAG:
                    multiply_round(r - PASS_LAG)
                for a in range(tests_a_round * j, tests_a_round * (j + 1)):
                    test_padding(x_words, c, a)
                if r == ROUNDS - 1:
                    valid_col = find_valid_tokens()
                operands = [quantise(x_rows4[:], ROWS, packed_held, "x")]
                for m in range(ROW_TILES):
                    operands.append(
                        quantise(
                            w_rows4[:, 4 * P * m : 4 * P * (m + 1)],
                            P,
                            packed_held if m == HELD_TILE else packed,
                            "w%d" % m,
                        )
                    )
                quantised.append(operands)
                r += 1
            if c + CHUNKS_AHEAD < len(CHUNK_WIDTHS):
                load_chunk(c + CHUNKS_AHEAD)

        for late_round in range(ROUNDS - PASS_LAG, ROUNDS - 1):
            multiply_round(late_round)

        b_flip = flip_pool.tile([P, P], F32, name="b_flip", tag="x_flip1")
        nc.tensor.transpose(b_flip[:], b_rows32[:], ident[:])
        valid_bank = flip_pool.tile([P, ROWS], F32, name="valid_bank", tag="x_flip0")
        for a in range(ROW_TILES):
            nc.tensor.matmul(
                out=valid_bank[:, P * a : P * (a + 1)],
                lhsT=valid_col[:, a : a + 1].to_broadcast([P, P]),
                rhs=ident[:],
                start=True,
                stop=True,
            )
        multiply_round(ROUNDS - 1)
        for held_round in range(ROUNDS - HELD, ROUNDS):
            multiply(quantised[held_round], held_round, HELD_TILE)

        bias_col = const.tile([P, ROW_TILES], F32, name="bias_col")
        nc.scalar.copy(out=bias_col[:], in_=b_flip[:, 0:ROW_TILES])
        valid = const.tile([P, SAMPLES, TOKENS], F32, name="valid")
        nc.scalar.copy(out=valid[:].rearrange("p s t -> p (s t)"), in_=valid_bank[:])
        n_valid = const.tile([P, SAMPLES], F32, name="n_valid")
        nc.vector.tensor_reduce(out=n_valid[:], in_=valid[:], axis=AX.X, op=ALU.add)
        n_floor = const.tile([P, 2, SAMPLES], F32, name="n_floor")
        nc.vector.tensor_scalar_max(out=n_floor[:, 0, :], in0=n_valid[:], scalar1=1.0)
        nc.vector.tensor_scalar(
            out=n_floor[:, 1, :], in0=n_valid[:], scalar1=-1.0, scalar2=1.0, op0=ALU.add, op1=ALU.max
        )
        n_inverse = const.tile([P, 2, SAMPLES], F32, name="n_inverse")
        nc.vector.reciprocal(out=n_inverse[:], in_=n_floor[:])

        stats = const.tile([P, SAMPLES, 2, ROW_TILES], F32, name="stats")
        variance = const.tile([P, SAMPLES, ROW_TILES], F32, name="variance")
        shape = [P, SAMPLES, TOKENS]

        y = []

        def gelu(m):
            y_m = tail.tile(shape, F32, name="y%d" % m, bufs=1)
            nc.scalar.activation(
                out=y_m[:].rearrange("p s t -> p (s t)"),
                in_=acc[m][:],
                func=ACT.Gelu,
                bias=bias_col[:, m : m + 1],
            )
            y.append(y_m)

        for m in range(HELD_TILE):
            gelu(m)

        def sum_of_squares(squares, m):
            total_sq = tail.tile([P, SAMPLES], F32, name="total_sq")
            nc.vector.tensor_reduce(out=total_sq[:], in_=squares[:], axis=AX.X, op=ALU.add)
            nc.vector.scalar_tensor_tensor(
                out=variance[:, :, m],
                in0=total_sq[:],
                scalar=SQRT_FLOOR,
                in1=n_inverse[:, 1, :],
                op0=ALU.max,
                op1=ALU.mult,
            )

        squares = [None] * ROW_TILES
        for m in range(ROW_TILES):
            kept = tail.tile(shape, F32, name="kept")
            nc.vector.tensor_tensor(out=kept[:], in0=y[m][:], in1=valid[:], op=ALU.mult)
            total_y = tail.tile([P, SAMPLES], F32, name="total_y")
            nc.vector.tensor_reduce(out=total_y[:], in_=kept[:], axis=AX.X, op=ALU.add)
            mean = stats[:, :, 1, m]
            nc.vector.tensor_tensor(out=mean, in0=total_y[:], in1=n_inverse[:, 0, :], op=ALU.mult)
            away = tail.tile(shape, F32, name="away")
            nc.vector.tensor_tensor(
                out=away[:], in0=y[m][:], in1=mean.unsqueeze(2).to_broadcast(shape), op=ALU.subtract
            )
            away_kept = tail.tile(shape, F32, name="away_kept")
            nc.vector.tensor_tensor(out=away_kept[:], in0=away[:], in1=valid[:], op=ALU.mult)
            squares[m] = tail.tile(shape, F32, name="squares")
            nc.scalar.activation(out=squares[m][:], in_=away_kept[:], func=ACT.Square)
            if m == HELD_TILE - 2:
                gelu(HELD_TILE)
                nc.scalar.activation(out=warm[:, 1:2], in_=one[:], func=ACT.Sqrt)
            if m > 0:
                sum_of_squares(squares[m - 1], m - 1)
        sum_of_squares(squares[ROW_TILES - 1], ROW_TILES - 1)

        root = const.tile([P, SAMPLES, ROW_TILES], F32, name="root")
        nc.scalar.activation(out=root[:], in_=variance[:], func=ACT.Sqrt)
        some = const.tile([P, SAMPLES, ROW_TILES], F32, name="some")
        nc.vector.tensor_single_scalar(out=some[:], in_=variance[:], scalar=SQRT_FLOOR, op=ALU.is_gt)
        nc.vector.tensor_tensor(out=stats[:, :, 0, :], in0=root[:], in1=some[:], op=ALU.mult)

        stats_bank = flip_pool.tile([P, P], F32, name="stats_bank", tag="w_flip0")
        nc.tensor.transpose(stats_bank[:], stats[:].rearrange("p s g m -> p (s g m)"), ident[:])
        result = const.tile([P, P], F32, name="result")
        nc.vector.tensor_copy(out=result[:], in_=stats_bank[:])
        nc.sync.dma_start(out=out.rearrange("s (g o) -> (s g) o", o=P), in_=result[:])
